import numpy as np
import ml_dtypes


def mxq(x, axis, fmt="e4m3"):
    dtype, down = {"e4m3": (ml_dtypes.float8_e4m3fn, 7), "e5m2": (ml_dtypes.float8_e5m2, 14)}[fmt]
    v = np.moveaxis(np.asarray(x, np.float32).astype(ml_dtypes.bfloat16).astype(np.float64), axis, -1)
    blocks = v.reshape(v.shape[:-1] + (-1, 32))
    amax = np.abs(blocks).max(-1, keepdims=True)
    byte = np.maximum(np.where(amax > 0, np.frexp(amax)[1] - 1 + 127, 0) - down, 1)
    scale = np.exp2(byte - 127.0)
    codes = (blocks / scale).astype(np.float32).astype(dtype).astype(np.float64)
    return np.moveaxis((codes * scale).reshape(v.shape), -1, axis)


WIDE = False


def mx_kscale(k):
    if not WIDE:
        return np.ones(k)
    levels = np.array([10, -10, 5, -5, 0])
    if k % 512:
        return np.exp2(np.random.permutation(np.resize(levels, k // 32))).repeat(32)
    a = np.empty((k // 512, 16))
    for p in range(k // 512):
        a[p, :8] = np.random.permutation(np.resize(levels, 8))
        for g in range(8):
            far = levels[np.abs(levels - a[p, g]) >= 10]
            a[p, g + 8] = far[np.random.randint(len(far))]
    return np.exp2(a.ravel()).repeat(32)


BF16 = ml_dtypes.bfloat16


def bf(x):
    return np.asarray(x, np.float32).astype(BF16)


def f64(x):
    return np.asarray(x).astype(np.float64)


N, E, G, M, H = 4096, 512, 512, 256, 1
HG = H * G


def sigmoid(v):
    return 1.0 / (1.0 + np.exp(-v))


def draw0():
    r = np.random.standard_normal
    s = mx_kscale(E)
    t = np.tile(mx_kscale(G), H)
    return {"q": bf(r((N, E)) * s),
            "rep": bf(r((N, E)) * s),
            "Wq": bf(r((E, HG)) * G ** 0.25 / np.sqrt(E) / s[:, None]),
            "Wk": bf(r((E, HG)) * G ** 0.25 / np.sqrt(E) / s[:, None]),
            "Wv": bf(r((E, HG)) / np.sqrt(E) / s[:, None] * t),
            "W1": bf(r((H, G, M)) * 2.0 / np.sqrt(G) / t.reshape(H, G, 1)),
            "b1": bf(r((H, M)) * 0.2)}


def core(q, rep, Wq, Wk, Wv, W1, b1):
    qq = mxq(f64(q), 1, "e4m3")
    rq = mxq(f64(rep), 1, "e4m3")
    Qh = (qq @ mxq(f64(Wq), 0, "e4m3")).reshape(N, H, G)
    Kh = (rq @ mxq(f64(Wk), 0, "e4m3")).reshape(N, H, G)
    Vh = (rq @ mxq(f64(Wv), 0, "e4m3")).reshape(N, H, G)
    gate = sigmoid(Qh * Kh * (1.0 / np.sqrt(G)))
    z = gate * Vh
    zt = z.transpose(1, 0, 2)
    pre = (mxq(zt, 2, "e4m3") @ mxq(f64(W1), 1, "e4m3")).transpose(1, 0, 2)
    return np.maximum(pre + f64(b1), 0.0)


def e4m3fn_bytes(y):
    return np.clip(np.asarray(y, np.float64), -448.0, 448.0).astype(np.float32).astype(ml_dtypes.float8_e4m3fn).view(np.uint8)


def e4m3fn_values(b):
    return np.asarray(b, np.uint8).view(ml_dtypes.float8_e4m3fn).astype(np.float64)


def setup_inputs():
    d = draw0()
    x0 = np.asarray(d['rep']).astype(np.float64)
    s = (np.max(np.abs(x0), axis=(0,), keepdims=True) / 448.0).astype(np.float32)
    out = {}
    for k, v in d.items():
        if k == 'rep':
            out['rep_bytes'] = e4m3fn_bytes(x0 / s.astype(np.float64))
            out['rep_scale'] = s
        else:
            out[k] = v
    return out


def reference(q, rep_bytes, rep_scale, Wq, Wk, Wv, W1, b1):
    return core(q, e4m3fn_values(rep_bytes) * rep_scale.astype(np.float64), Wq, Wk, Wv, W1, b1)

@@ -1,0 +1,281 @@
+from contextlib import ExitStack
+
+import concourse.mybir as mybir
+from concourse.masks import make_identity
+
+N, E, G, M = 4096, 512, 512, 256
+FLOPS = 2 * N * E * G * 3 + 2 * N * G * M
+
+F32 = mybir.dt.float32
+BF16 = mybir.dt.bfloat16
+U32 = mybir.dt.uint32
+U8 = mybir.dt.uint8
+FP8 = mybir.dt.float8_e4m3fn
+FP8X4 = mybir.dt.float8_e4m3fn_x4
+ACT = mybir.ActivationFunctionType
+MULT = mybir.AluOpType.mult
+
+P = 128
+PACK = 4
+UNIT = 128
+BLOCK = 2 * UNIT
+BLOCKS = N // BLOCK
+GROUPS = (256, 256, 512, 1024, 1024, 1024)
+
+
+def tile_treehopnode_pa_t_kernel(tc, q, rep_bytes, rep_scale, Wq, Wk, Wv, W1, b1, out):
+    nc = tc.nc
+    with ExitStack() as ctx:
+        keep = ctx.enter_context(tc.tile_pool(name="keep", bufs=1))
+        work = ctx.enter_context(tc.tile_pool(name="work", bufs=2))
+        psum = ctx.enter_context(tc.psum_pool(name="psum", bufs=1))
+
+        ident = keep.tile([P, P], F32, name="ident")
+        make_identity(nc, ident[:])
+        warm = keep.tile([P, 1], F32, name="warm")
+        nc.vector.memset(warm[:], 0.0)
+        warm_out = keep.tile([P, 1], F32, name="warm_out")
+
+        ctx.enter_context(tc.manual_schedule())
+        nc.scalar.activation(warm_out[:], warm[:], ACT.Sigmoid)
+
+        scol = keep.tile([P, PACK], F32, name="scol")
+        nc.sync.dma_start(out=scol[:], in_=rep_scale.rearrange("o (p t) -> p (o t)", t=PACK))
+        q_in, r_in, where = [], [], []
+        start = 0
+        for g, tokens in enumerate(GROUPS):
+            rows = tokens // P
+            q_in.append(keep.tile([P, rows * E], BF16, name="q_in%d" % g, align_bytes=64))
+            r_in.append(keep.tile([P, rows * E], U8, name="r_in%d" % g, align_bytes=64))
+            for i in range(0, rows, 2):
+                where.append((g, i, start, rows))
+            start += tokens
+
+        def load_rep(g):
+            first = sum(GROUPS[:g])
+            src = rep_bytes[first:first + GROUPS[g], :].rearrange("(p i) k -> p (i k)", p=P)
+            nc.sync.dma_start(out=r_in[g][:], in_=src)
+
+        def load_q(g):
+            first = sum(GROUPS[:g])
+            src = q[first:first + GROUPS[g], :].rearrange("(p i) k -> p (i k)", p=P)
+            nc.sync.dma_start(out=q_in[g][:], in_=src)
+
+        raw = {}
+
+        def load_w(key, src):
+            width = src.shape[1]
+            raw[key] = keep.tile([P, PACK, width], BF16, name="raw_" + key, align_bytes=64)
+            nc.sync.dma_start(out=raw[key][:], in_=src.rearrange("(p j) c -> p j c", j=PACK))
+
+        load_rep(0)
+        load_q(0)
+        load_w("q", Wq)
+        load_w("k", Wk)
+        load_rep(1)
+        load_q(1)
+        load_w("v", Wv)
+        bias = keep.tile([P, 2], BF16, name="bias")
+        nc.sync.dma_start(out=bias[:], in_=b1.rearrange("o (p c) -> p (o c)", c=2))
+        load_w("1", W1.rearrange("h k m -> (h k) m"))
+        for g in range(2, len(GROUPS)):
+            load_rep(g)
+            load_q(g)
+
+        grouped, wc, ws = {}, {}, {}
+
+        def weight_group(key, eng):
+            width = raw[key].shape[2]
+            parts = width // P
+            grouped[key] = keep.tile([P, width * PACK], BF16, name="grouped_" + key, align_bytes=64)
+            dst = grouped[key][:].rearrange("p (t m j) -> p t m j", t=parts, j=PACK)
+            src = raw[key][:].rearrange("p j (m t) -> p t m j", t=parts)
+            eng(out=dst, in_=src)
+
+        def weight_quantize(key):
+            width = raw[key].shape[2]
+            wc[key] = keep.tile([P, width], U32, name="wc_" + key, align_bytes=64)
+            ws[key] = keep.tile([P, width], U8, name="ws_" + key, align_bytes=64)
+            nc.vector.quantize_mx(out=wc[key][:].bitcast(FP8X4), scales=ws[key][:], in_=grouped[key][:])
+
+        def mx(dst, key, col, codes, scales, tok, n):
+            nc.tensor.matmul_mx(
+                out=dst,
+                lhsT=wc[key][:, col * P:(col + 1) * P].bitcast(FP8X4),
+                lhsT_scale=ws[key][:, col * P:(col + 1) * P],
+                rhs=codes[:, tok:tok + n].bitcast(FP8X4),
+                rhs_scale=scales[:, tok:tok + n],
+                start=True,
+                stop=True,
+            )
+
+        sc_ps = psum.tile([P, PACK, P], F32, name="sc_ps", tag="tr")
+        for t in range(PACK):
+            nc.tensor.transpose(sc_ps[:, t, :], scol[:, t:t + 1].to_broadcast([P, P]), ident[:])
+        sc_bc = keep.tile([P, 2, E], F32, name="sc_bc", align_bytes=64)
+        sc_view = sc_ps[:].rearrange("p t n -> p n t")
+        nc.vector.tensor_copy(out=sc_bc[:, 0, :].rearrange("p (n t) -> p n t", t=PACK), in_=sc_view)
+        nc.scalar.copy(out=sc_bc[:, 1, :].rearrange("p (n t) -> p n t", t=PACK), in_=sc_view)
+
+        live = {}
+
+        def widen(b):
+            g, i, first, rows = where[b]
+            x = work.tile([P, 2 * E], BF16, name="x", tag="x", align_bytes=64)
+            nc.vector.tensor_tensor(
+                out=x[:],
+                in0=r_in[g][:, i * E:(i + 2) * E].bitcast(FP8),
+                in1=sc_bc[:].rearrange("p i k -> p (i k)"),
+                op=MULT,
+            )
+            live["x", b] = x[:].bitcast(F32)
+
+        def turn(words, tag):
+            bank = psum.tile([P, 2, 2, P], F32, name="bank_" + tag, tag=tag)
+            half = E // 2
+            for i in range(2):
+                for u in range(2):
+                    nc.tensor.transpose(bank[:, i, u, :], words[:, i * half + u:(i + 1) * half:2], ident[:])
+            return bank
+
+        def turn_rep(b):
+            live["tr", b] = turn(live.pop(("x", b)), "tr")
+
+        def turn_q(b):
+            g, i, first, rows = where[b]
+            live["tq", b] = turn(q_in[g][:, i * E:(i + 2) * E].bitcast(F32), "tq")
+
+        def collect(b, kind):
+            bank = live.pop(("t" + kind, b))
+            g = work.tile([P, BLOCK * PACK], BF16, name="g" + kind, tag="g" + kind, align_bytes=64)
+            nc.scalar.copy(
+                out=g[:].bitcast(F32).rearrange("p (i r u) -> p i r u", i=2, u=2),
+                in_=bank[:].rearrange("p i u r -> p i r u"),
+            )
+            live["g" + kind, b] = g
+
+        def quantize(b, kind):
+            g = live.pop(("g" + kind, b))
+            codes = work.tile([P, BLOCK], U32, name="c" + kind, tag="c" + kind, align_bytes=64)
+            scales = work.tile([P, BLOCK], U8, name="s" + kind, tag="s" + kind, align_bytes=64)
+            nc.vector.quantize_mx(out=codes[:].bitcast(FP8X4), scales=scales[:], in_=g[:])
+            live["c" + kind, b] = (codes, scales)
+
+        def project(b, unit, key, kind):
+            codes, scales = live["c" + kind, b]
+            bank = psum.tile([P, PACK, UNIT], F32, name="bank_" + key, tag="qkv", bufs=4)
+            for t in range(PACK):
+                mx(bank[:, t, :], key, t, codes, scales, unit * UNIT, UNIT)
+            live[key, b, unit] = bank[:].rearrange("p t n -> p n t")
+
+        def copy_q(b, unit):
+            t = work.tile([P, UNIT, PACK], F32, name="q_sb", tag="q_sb", bufs=3, align_bytes=64)
+            nc.scalar.copy(out=t[:], in_=live.pop(("q", b, unit)))
+            live["qs", b, unit] = t
+
+        def times_k(b, unit):
+            t = work.tile([P, UNIT, PACK], F32, name="qk", tag="qk", bufs=3, align_bytes=64)
+            nc.vector.tensor_tensor(out=t[:], in0=live.pop(("k", b, unit)), in1=live.pop(("qs", b, unit))[:], op=MULT)
+            live["qk", b, unit] = t
+
+        def gate(b, unit):
+            t = work.tile([P, UNIT, PACK], F32, name="gate", tag="gate", bufs=3, align_bytes=64)
+            nc.scalar.activation(t[:], live.pop(("qk", b, unit))[:], ACT.Sigmoid, scale=G ** -0.5)
+            live["gate", b, unit] = t
+
+        def times_v(b, unit):
+            if unit == 0:
+                live["gz", b] = work.tile([P, BLOCK * PACK], BF16, name="gz", tag="gz", align_bytes=64)
+            half = UNIT * PACK
+            dst = live["gz", b][:, unit * half:(unit + 1) * half].rearrange("p (n t) -> p n t", t=PACK)
+            nc.vector.tensor_tensor(out=dst, in0=live.pop(("v", b, unit)), in1=live.pop(("gate", b, unit))[:], op=MULT)
+
+        def layer(b):
+            codes, scales = live.pop(("cz", b))
+            bank = psum.tile([P, 2, BLOCK], F32, name="bank_o", tag="o")
+            for c in range(2):
+                mx(bank[:, c, :], "1", c, codes, scales, 0, BLOCK)
+            live["o", b] = bank
+
+        def relu(b):
+            bank = live.pop(("o", b))
+            t = work.tile([P, 2, BLOCK], F32, name="act", tag="act", align_bytes=64)
+            for c in range(2):
+                nc.scalar.activation(t[:, c, :], bank[:, c, :], ACT.Relu, bias=bias[:, c:c + 1])
+            live["act", b] = t
+
+        def turn_back(b):
+            t = live.pop(("act", b))
+            bank = psum.tile([P, 2, 2, P], F32, name="bank_b", tag="back")
+            for i in range(2):
+                for c in range(2):
+                    nc.tensor.transpose(bank[:, i, c, :], t[:, c, i * UNIT:(i + 1) * UNIT], ident[:])
+            live["back", b] = bank
+
+        def store(b):
+            g, i, first, rows = where[b]
+            bank = live.pop(("back", b))
+            t = work.tile([P, 2, M], F32, name="res", tag="res", bufs=3, align_bytes=64)
+            nc.scalar.copy(
+                out=t[:].rearrange("p i (m c) -> p i m c", c=2),
+                in_=bank[:].rearrange("p i c m -> p i m c"),
+            )
+            dst = out[first:first + rows * P, :, :].rearrange("(p i) o m -> p i (o m)", p=P)
+            nc.sync.dma_start(out=dst[:, i:i + 2, :], in_=t[:])
+
+        def on(b):
+            return 0 <= b < BLOCKS
+
+        for s in range(-3, BLOCKS + 2):
+            if on(s - 1):
+                layer(s - 1)
+            if on(s):
+                copy_q(s, 0)
+                copy_q(s, 1)
+            if s == -2:
+                weight_group("q", nc.vector.tensor_copy)
+                weight_group("k", nc.vector.tensor_copy)
+                weight_quantize("q")
+                weight_quantize("k")
+            if on(s):
+                project(s, 0, "v", "r")
+                project(s, 1, "v", "r")
+                times_k(s, 0)
+                times_k(s, 1)
+            if on(s + 1):
+                collect(s + 1, "q")
+            if s == -1:
+                weight_group("v", nc.scalar.copy)
+            if on(s + 2):
+                turn_rep(s + 2)
+                turn_q(s + 2)
+            if on(s - 2):
+                turn_back(s - 2)
+            if on(s + 1):
+                quantize(s + 1, "q")
+                quantize(s + 1, "r")
+            if on(s):
+                gate(s, 0)
+                gate(s, 1)
+                times_v(s, 0)
+                times_v(s, 1)
+            if on(s + 2):
+                collect(s + 2, "r")
+            if on(s + 1):
+                for key, kind in (("q", "q"), ("k", "r")):
+                    for unit in range(2):
+                        project(s + 1, unit, key, kind)
+            if on(s - 1):
+                relu(s - 1)
+            if on(s - 2):
+                store(s - 2)
+            if on(s + 3):
+                widen(s + 3)
+            if s == -1:
+                weight_quantize("v")
+            if s == 0:
+                weight_group("1", nc.vector.tensor_copy)
+            if on(s):
+                quantize(s, "z")
+            if s == 0:
+                weight_quantize("1")

@@ -109,25 +109,30 @@ def tile_treehopnode_pa_t_kernel(tc, q, rep_bytes, rep_scale, Wq, Wk, Wv, W1, b1
                 stop=True,
             )
 
-        sc_ps = psum.tile([P, PACK, P], F32, name="sc_ps", tag="tr")
-        for t in range(PACK):
-            nc.tensor.transpose(sc_ps[:, t, :], scol[:, t:t + 1].to_broadcast([P, P]), ident[:])
-        sc_bc = keep.tile([P, 2, E], F32, name="sc_bc", align_bytes=64)
-        sc_view = sc_ps[:].rearrange("p t n -> p n t")
-        nc.vector.tensor_copy(out=sc_bc[:, 0, :].rearrange("p (n t) -> p n t", t=PACK), in_=sc_view)
-        nc.scalar.copy(out=sc_bc[:, 1, :].rearrange("p (n t) -> p n t", t=PACK), in_=sc_view)
+        bias_bc = keep.tile([P, 2, M], F32, name="bias_bc", align_bytes=64)
+        bias32 = keep.tile([P, 2], F32, name="bias32")
+
+        def spread_bias():
+            nc.scalar.copy(out=bias32[:], in_=bias[:])
+            bank = psum.tile([P, 2, P], F32, name="bank_bias", tag="back")
+            for c in range(2):
+                nc.tensor.transpose(bank[:, c, :], bias32[:, c:c + 1].to_broadcast([P, P]), ident[:])
+            for i in range(2):
+                nc.scalar.copy(
+                    out=bias_bc[:, i, :].rearrange("p (m c) -> p m c", c=2),
+                    in_=bank[:].rearrange("p c m -> p m c"),
+                )
 
         live = {}
 
         def widen(b):
             g, i, first, rows = where[b]
             x = work.tile([P, 2 * E], BF16, name="x", tag="x", align_bytes=64)
-            nc.vector.tensor_tensor(
-                out=x[:],
-                in0=r_in[g][:, i * E:(i + 2) * E].bitcast(FP8),
-                in1=sc_bc[:].rearrange("p i k -> p (i k)"),
-                op=MULT,
-            )
+            for h in range(2):
+                nc.gpsimd.tensor_copy(
+                    out=x[:, h * E:(h + 1) * E],
+                    in_=r_in[g][:, (i + h) * E:(i + h + 1) * E].bitcast(FP8),
+                )
             live["x", b] = x[:].bitcast(F32)
 
         def turn(words, tag):
@@ -135,7 +140,7 @@ def tile_treehopnode_pa_t_kernel(tc, q, rep_bytes, rep_scale, Wq, Wk, Wv, W1, b1
             half = E // 2
             for i in range(2):
                 for u in range(2):
-                    nc.tensor.transpose(bank[:, i, u, :], words[:, i * half + u:(i + 1) * half:2], ident[:])
+                    nc.tensor.transpose(bank[:, u, i, :], words[:, i * half + u:(i + 1) * half:2], ident[:])
             return bank
 
         def turn_rep(b):
@@ -147,55 +152,119 @@ def tile_treehopnode_pa_t_kernel(tc, q, rep_bytes, rep_scale, Wq, Wk, Wv, W1, b1
 
         def collect(b, kind):
             bank = live.pop(("t" + kind, b))
-            g = work.tile([P, BLOCK * PACK], BF16, name="g" + kind, tag="g" + kind, align_bytes=64)
-            nc.scalar.copy(
-                out=g[:].bitcast(F32).rearrange("p (i r u) -> p i r u", i=2, u=2),
-                in_=bank[:].rearrange("p i u r -> p i r u"),
-            )
-            live["g" + kind, b] = g
+            if kind == "q":
+                live["gqr", b] = work.tile([P, 2 * BLOCK * PACK], BF16, name="gqr", tag="gqr", align_bytes=64)
+            k = "qr".index(kind)
+            dst = live["gqr", b][:, k * BLOCK * PACK:(k + 1) * BLOCK * PACK]
+            if kind == "q":
+                nc.scalar.copy(
+                    out=dst.bitcast(F32).rearrange("p (n u) -> p n u", u=2),
+                    in_=bank[:].rearrange("p u i r -> p (i r) u"),
+                )
+            else:
+                nc.vector.tensor_tensor(
+                    out=dst.rearrange("p (n u e) -> p n u e", u=2, e=2),
+                    in0=bank[:].rearrange("p u i r -> p u (i r)").bitcast(BF16).rearrange("p u (n e) -> p n u e", e=2),
+                    in1=scol[:].rearrange("p (u e) -> p u e", e=2).unsqueeze(1).to_broadcast([P, BLOCK, 2, 2]),
+                    op=MULT,
+                )
 
-        def quantize(b, kind):
-            g = live.pop(("g" + kind, b))
-            codes = work.tile([P, BLOCK], U32, name="c" + kind, tag="c" + kind, align_bytes=64)
-            scales = work.tile([P, BLOCK], U8, name="s" + kind, tag="s" + kind, align_bytes=64)
+        def quantize_qr(b):
+            g = live.pop(("gqr", b))
+            codes = work.tile([P, 2 * BLOCK], U32, name="cqr", tag="cqr", bufs=3, align_bytes=64)
+            scales = work.tile([P, 2 * BLOCK], U8, name="sqr", tag="sqr", bufs=3, align_bytes=64)
             nc.vector.quantize_mx(out=codes[:].bitcast(FP8X4), scales=scales[:], in_=g[:])
-            live["c" + kind, b] = (codes, scales)
+            live["cqr", b] = (codes, scales)
 
-        def project(b, unit, key, kind):
-            codes, scales = live["c" + kind, b]
-            bank = psum.tile([P, PACK, UNIT], F32, name="bank_" + key, tag="qkv", bufs=4)
-            for t in range(PACK):
-                mx(bank[:, t, :], key, t, codes, scales, unit * UNIT, UNIT)
-            live[key, b, unit] = bank[:].rearrange("p t n -> p n t")
+        def quantize_z(b):
+            g = live.pop(("gz", b))
+            codes = work.tile([P, BLOCK], U32, name="cz", tag="cz", align_bytes=64)
+            scales = work.tile([P, BLOCK], U8, name="sz", tag="sz", align_bytes=64)
+            nc.vector.quantize_mx(out=codes[:].bitcast(FP8X4), scales=scales[:], in_=g[:])
+            live["cz", b] = (codes, scales)
 
-        def copy_q(b, unit):
-            t = work.tile([P, UNIT, PACK], F32, name="q_sb", tag="q_sb", bufs=3, align_bytes=64)
-            nc.scalar.copy(out=t[:], in_=live.pop(("q", b, unit)))
-            live["qs", b, unit] = t
+        def project(b, key):
+            codes, scales = live["cqr", b]
+            base = 0 if key == "q" else BLOCK
+            for unit in range(2):
+                bank = psum.tile([P, PACK, UNIT], F32, name="bank_qkv", tag="qkv", bufs=4)
+                for t in range(PACK):
+                    mx(bank[:, t, :], key, t, codes, scales, base + unit * UNIT, UNIT)
+                live[key, b, unit] = bank[:].rearrange("p t n -> p n t")
 
-        def times_k(b, unit):
-            t = work.tile([P, UNIT, PACK], F32, name="qk", tag="qk", bufs=3, align_bytes=64)
-            nc.vector.tensor_tensor(out=t[:], in0=live.pop(("k", b, unit)), in1=live.pop(("qs", b, unit))[:], op=MULT)
-            live["qk", b, unit] = t
+        def copy_q(b):
+            for unit in range(2):
+                t = work.tile([P, UNIT, PACK], F32, name="q_sb", tag="q_sb", bufs=4, align_bytes=64)
+                nc.scalar.copy(out=t[:], in_=live.pop(("q", b, unit)))
+                live["qs", b, unit] = t
 
-        def gate(b, unit):
-            t = work.tile([P, UNIT, PACK], F32, name="gate", tag="gate", bufs=3, align_bytes=64)
-            nc.scalar.activation(t[:], live.pop(("qk", b, unit))[:], ACT.Sigmoid, scale=G ** -0.5)
-            live["gate", b, unit] = t
+        def times_k(b):
+            t = work.tile([P, 2, UNIT, PACK], F32, name="qk", tag="qk", align_bytes=64)
+            for unit in range(2):
+                nc.vector.tensor_tensor(out=t[:, unit, :, :], in0=live.pop(("k", b, unit)), in1=live.pop(("qs", b, unit))[:], op=MULT)
+            live["qk", b] = t
 
-        def times_v(b, unit):
-            if unit == 0:
-                live["gz", b] = work.tile([P, BLOCK * PACK], BF16, name="gz", tag="gz", align_bytes=64)
+        def gate(b):
+            t = work.tile([P, 2, UNIT, PACK], F32, name="gate", tag="gate", align_bytes=64)
+            nc.scalar.activation(
+                t[:].rearrange("p i n t -> p (i n t)"),
+                live.pop(("qk", b))[:].rearrange("p i n t -> p (i n t)"),
+                ACT.Sigmoid, scale=G ** -0.5)
+            live["gate", b] = t
+
+        def times_v(b):
+            z = work.tile([P, BLOCK * PACK], BF16, name="gz", tag="gz", align_bytes=64)
+            t = live.pop(("gate", b))
             half = UNIT * PACK
-            dst = live["gz", b][:, unit * half:(unit + 1) * half].rearrange("p (n t) -> p n t", t=PACK)
-            nc.vector.tensor_tensor(out=dst, in0=live.pop(("v", b, unit)), in1=live.pop(("gate", b, unit))[:], op=MULT)
+            for unit in range(2):
+                dst = z[:, unit * half:(unit + 1) * half].rearrange("p (n t) -> p n t", t=PACK)
+                nc.vector.tensor_tensor(out=dst, in0=live.pop(("v", b, unit)), in1=t[:, unit, :, :], op=MULT)
+            live["gz", b] = z
+
+        def straight(b):
+            return b == BLOCKS - 1
 
         def layer(b):
             codes, scales = live.pop(("cz", b))
             bank = psum.tile([P, 2, BLOCK], F32, name="bank_o", tag="o")
             for c in range(2):
-                mx(bank[:, c, :], "1", c, codes, scales, 0, BLOCK)
+                if straight(b):
+                    nc.tensor.matmul_mx(
+                        out=bank[:, c, :],
+                        lhsT=codes[:, c * UNIT:(c + 1) * UNIT].bitcast(FP8X4),
+                        lhsT_scale=scales[:, c * UNIT:(c + 1) * UNIT],
+                        rhs=wc["1"][:].bitcast(FP8X4),
+                        rhs_scale=ws["1"][:],
+                        start=True,
+                        stop=True,
+                    )
+                else:
+                    mx(bank[:, c, :], "1", c, codes, scales, 0, BLOCK)
             live["o", b] = bank
+
+        def add_bias(b):
+            bank = live.pop(("o", b))
+            t = work.tile([P, 2, M], F32, name="pre", tag="pre", align_bytes=64)
+            nc.vector.tensor_tensor(
+                out=t[:].rearrange("p i (m c) -> p i m c", c=2),
+                in0=bank[:].rearrange("p i (c m) -> p i m c", c=2),
+                in1=bias_bc[:].rearrange("p i (m c) -> p i m c", c=2),
+                op=mybir.AluOpType.add,
+            )
+            live["pre", b] = t
+
+        def send(b, t):
+            g, i, first, rows = where[b]
+            dst = out[first:first + rows * P, :, :].rearrange("(p i) o m -> p i (o m)", p=P)
+            nc.sync.dma_start(out=dst[:, i:i + 2, :], in_=t[:])
+
+        def relu_straight(b):
+            t = work.tile([P, 2, M], F32, name="res", tag="res", bufs=3, align_bytes=64)
+            nc.scalar.activation(
+                t[:].rearrange("p i m -> p (i m)"),
+                live.pop(("pre", b))[:].rearrange("p i m -> p (i m)"),
+                ACT.Relu)
+            send(b, t)
 
         def relu(b):
             bank = live.pop(("o", b))
@@ -213,69 +282,70 @@ def tile_treehopnode_pa_t_kernel(tc, q, rep_bytes, rep_scale, Wq, Wk, Wv, W1, b1
             live["back", b] = bank
 
         def store(b):
-            g, i, first, rows = where[b]
             bank = live.pop(("back", b))
             t = work.tile([P, 2, M], F32, name="res", tag="res", bufs=3, align_bytes=64)
             nc.scalar.copy(
                 out=t[:].rearrange("p i (m c) -> p i m c", c=2),
                 in_=bank[:].rearrange("p i c m -> p i m c"),
             )
-            dst = out[first:first + rows * P, :, :].rearrange("(p i) o m -> p i (o m)", p=P)
-            nc.sync.dma_start(out=dst[:, i:i + 2, :], in_=t[:])
+            send(b, t)
 
         def on(b):
             return 0 <= b < BLOCKS
 
-        for s in range(-3, BLOCKS + 2):
-            if on(s - 1):
-                layer(s - 1)
+        for s in range(-4, BLOCKS + 4):
+            if s == -4:
+                weight_group("q", nc.scalar.copy)
             if on(s):
-                copy_q(s, 0)
-                copy_q(s, 1)
-            if s == -2:
-                weight_group("q", nc.vector.tensor_copy)
-                weight_group("k", nc.vector.tensor_copy)
-                weight_quantize("q")
-                weight_quantize("k")
-            if on(s):
-                project(s, 0, "v", "r")
-                project(s, 1, "v", "r")
-                times_k(s, 0)
-                times_k(s, 1)
+                times_k(s)
             if on(s + 1):
-                collect(s + 1, "q")
-            if s == -1:
-                weight_group("v", nc.scalar.copy)
+                project(s + 1, "q")
             if on(s + 2):
-                turn_rep(s + 2)
-                turn_q(s + 2)
-            if on(s - 2):
-                turn_back(s - 2)
-            if on(s + 1):
-                quantize(s + 1, "q")
-                quantize(s + 1, "r")
-            if on(s):
-                gate(s, 0)
-                gate(s, 1)
-                times_v(s, 0)
-                times_v(s, 1)
-            if on(s + 2):
+                collect(s + 2, "q")
                 collect(s + 2, "r")
-            if on(s + 1):
-                for key, kind in (("q", "q"), ("k", "r")):
-                    for unit in range(2):
-                        project(s + 1, unit, key, kind)
             if on(s - 1):
-                relu(s - 1)
-            if on(s - 2):
-                store(s - 2)
+                times_v(s - 1)
+            if on(s - 2) and straight(s - 2):
+                add_bias(s - 2)
             if on(s + 3):
-                widen(s + 3)
+                turn_rep(s + 3)
+            if on(s):
+                gate(s)
+            if on(s + 1):
+                project(s + 1, "k")
+            if on(s + 2):
+                quantize_qr(s + 2)
+            if on(s + 1):
+                copy_q(s + 1)
+            if on(s + 3):
+                turn_q(s + 3)
+            if on(s - 3) and not straight(s - 3):
+                turn_back(s - 3)
+            if on(s):
+                project(s, "v")
+            if on(s - 1):
+                quantize_z(s - 1)
+            if on(s + 4):
+                widen(s + 4)
+            if s == -4:
+                weight_group("k", nc.vector.tensor_copy)
+            if s == -3:
+                weight_quantize("q")
+            if s == -2:
+                weight_quantize("k")
+                weight_group("v", nc.scalar.copy)
             if s == -1:
                 weight_quantize("v")
             if s == 0:
                 weight_group("1", nc.vector.tensor_copy)
-            if on(s):
-                quantize(s, "z")
-            if s == 0:
                 weight_quantize("1")
+                spread_bias()
+            if on(s - 2):
+                if straight(s - 2):
+                    relu_straight(s - 2)
+                else:
+                    relu(s - 2)
+            if on(s - 1):
+                layer(s - 1)
+            if on(s - 3) and not straight(s - 3):
+                store(s - 3)

@@ -40,7 +40,7 @@ def tile_treehopnode_pa_t_kernel(tc, q, rep_bytes, rep_scale, Wq, Wk, Wv, W1, b1
         nc.scalar.activation(warm_out[:], warm[:], ACT.Sigmoid)
 
         scol = keep.tile([P, PACK], F32, name="scol")
-        nc.sync.dma_start(out=scol[:], in_=rep_scale.rearrange("o (p t) -> p (o t)", t=PACK))
+        bias = keep.tile([P, 2], BF16, name="bias")
         q_in, r_in, where = [], [], []
         start = 0
         for g, tokens in enumerate(GROUPS):
@@ -61,36 +61,33 @@ def tile_treehopnode_pa_t_kernel(tc, q, rep_bytes, rep_scale, Wq, Wk, Wv, W1, b1
             src = q[first:first + GROUPS[g], :].rearrange("(p i) k -> p (i k)", p=P)
             nc.sync.dma_start(out=q_in[g][:], in_=src)
 
-        raw = {}
+        raw, grouped, wc, ws = {}, {}, {}, {}
 
         def load_w(key, src):
             width = src.shape[1]
             raw[key] = keep.tile([P, PACK, width], BF16, name="raw_" + key, align_bytes=64)
+            grouped[key] = keep.tile([P, width * PACK], BF16, name="grouped_" + key, align_bytes=64)
             nc.sync.dma_start(out=raw[key][:], in_=src.rearrange("(p j) c -> p j c", j=PACK))
 
+        nc.sync.dma_start(out=scol[:], in_=rep_scale.rearrange("o (p t) -> p (o t)", t=PACK))
         load_rep(0)
         load_q(0)
         load_w("q", Wq)
-        load_w("k", Wk)
         load_rep(1)
         load_q(1)
+        load_w("k", Wk)
         load_w("v", Wv)
-        bias = keep.tile([P, 2], BF16, name="bias")
         nc.sync.dma_start(out=bias[:], in_=b1.rearrange("o (p c) -> p (o c)", c=2))
         load_w("1", W1.rearrange("h k m -> (h k) m"))
         for g in range(2, len(GROUPS)):
             load_rep(g)
             load_q(g)
 
-        grouped, wc, ws = {}, {}, {}
-
-        def weight_group(key, eng):
-            width = raw[key].shape[2]
-            parts = width // P
-            grouped[key] = keep.tile([P, width * PACK], BF16, name="grouped_" + key, align_bytes=64)
+        def weight_group(key, copy, first=0, last=4):
+            parts = raw[key].shape[2] // P
             dst = grouped[key][:].rearrange("p (t m j) -> p t m j", t=parts, j=PACK)
             src = raw[key][:].rearrange("p j (m t) -> p t m j", t=parts)
-            eng(out=dst, in_=src)
+            copy(out=dst[:, first:last, :, :], in_=src[:, first:last, :, :])
 
         def weight_quantize(key):
             width = raw[key].shape[2]
@@ -109,8 +106,18 @@ def tile_treehopnode_pa_t_kernel(tc, q, rep_bytes, rep_scale, Wq, Wk, Wv, W1, b1
                 stop=True,
             )
 
+        sc_bc = keep.tile([P, E], F32, name="sc_bc", align_bytes=64)
         bias_bc = keep.tile([P, 2, M], F32, name="bias_bc", align_bytes=64)
         bias32 = keep.tile([P, 2], F32, name="bias32")
+
+        def spread_scale():
+            bank = psum.tile([P, PACK, P], F32, name="bank_sc", tag="back")
+            for t in range(PACK):
+                nc.tensor.transpose(bank[:, t, :], scol[:, t:t + 1].to_broadcast([P, P]), ident[:])
+            nc.vector.tensor_copy(
+                out=sc_bc[:].rearrange("p (n t) -> p n t", t=PACK),
+                in_=bank[:].rearrange("p t n -> p n t"),
+            )
 
         def spread_bias():
             nc.scalar.copy(out=bias32[:], in_=bias[:])
@@ -125,14 +132,24 @@ def tile_treehopnode_pa_t_kernel(tc, q, rep_bytes, rep_scale, Wq, Wk, Wv, W1, b1
 
         live = {}
 
+        def shared(b):
+            return b in (4,6,8,10,12,14)
+
+        def straight(b):
+            return b in (14,15,)
+
         def widen(b):
             g, i, first, rows = where[b]
-            x = work.tile([P, 2 * E], BF16, name="x", tag="x", align_bytes=64)
+            x = work.tile([P, 2 * E], BF16, name="x", tag="x", bufs=3, align_bytes=64)
             for h in range(2):
-                nc.gpsimd.tensor_copy(
-                    out=x[:, h * E:(h + 1) * E],
-                    in_=r_in[g][:, (i + h) * E:(i + h + 1) * E].bitcast(FP8),
-                )
+                dst = x[:, h * E:(h + 1) * E]
+                if h == 1 and shared(b):
+                    dst = work.tile([P, E], BF16, name="plain", tag="plain", align_bytes=64)[:]
+                nc.gpsimd.tensor_copy(out=dst, in_=r_in[g][:, (i + h) * E:(i + h + 1) * E].bitcast(FP8))
+            if shared(b):
+                for c in range(2):
+                    cols = slice(c * E // 2, (c + 1) * E // 2)
+                    nc.gpsimd.tensor_tensor(out=x[:, E + c * E // 2:E + (c + 1) * E // 2], in0=dst[:, cols], in1=sc_bc[:, cols], op=MULT)
             live["x", b] = x[:].bitcast(F32)
 
         def turn(words, tag):
@@ -150,30 +167,39 @@ def tile_treehopnode_pa_t_kernel(tc, q, rep_bytes, rep_scale, Wq, Wk, Wv, W1, b1
             g, i, first, rows = where[b]
             live["tq", b] = turn(q_in[g][:, i * E:(i + 2) * E].bitcast(F32), "tq")
 
-        def collect(b, kind):
-            bank = live.pop(("t" + kind, b))
-            if kind == "q":
-                live["gqr", b] = work.tile([P, 2 * BLOCK * PACK], BF16, name="gqr", tag="gqr", align_bytes=64)
-            k = "qr".index(kind)
-            dst = live["gqr", b][:, k * BLOCK * PACK:(k + 1) * BLOCK * PACK]
-            if kind == "q":
-                nc.scalar.copy(
-                    out=dst.bitcast(F32).rearrange("p (n u) -> p n u", u=2),
-                    in_=bank[:].rearrange("p u i r -> p (i r) u"),
-                )
-            else:
-                nc.vector.tensor_tensor(
-                    out=dst.rearrange("p (n u e) -> p n u e", u=2, e=2),
-                    in0=bank[:].rearrange("p u i r -> p u (i r)").bitcast(BF16).rearrange("p u (n e) -> p n u e", e=2),
-                    in1=scol[:].rearrange("p (u e) -> p u e", e=2).unsqueeze(1).to_broadcast([P, BLOCK, 2, 2]),
-                    op=MULT,
-                )
+        def grouped_tile(b):
+            if ("gqr", b) not in live:
+                live["gqr", b] = work.tile([P, 2, BLOCK * PACK], BF16, name="gqr", tag="gqr", align_bytes=64)
+            return live["gqr", b]
+
+        def copy_words(dst, bank, first, last):
+            nc.scalar.copy(
+                out=dst[:, first * P * PACK:last * P * PACK].bitcast(F32).rearrange("p (i r u) -> p i r u", r=P, u=2),
+                in_=bank[:, :, first:last, :].rearrange("p u i r -> p i r u"),
+            )
+
+        def collect_q(b):
+            copy_words(grouped_tile(b)[:, 0, :], live.pop(("tq", b)), 0, 2)
+
+        def scale_rep(b):
+            bank = live.pop(("tr", b))
+            dst = grouped_tile(b)[:, 1, :]
+            n = P if shared(b) else 2 * P
+            words = bank[:].rearrange("p u i r -> p u (i r)")[:, :, 0:n]
+            nc.vector.tensor_tensor(
+                out=dst[:, 0:n * PACK].rearrange("p (n u e) -> p n u e", u=2, e=2),
+                in0=words.bitcast(BF16).rearrange("p u (n e) -> p n u e", e=2),
+                in1=scol[:].rearrange("p (u e) -> p u e", e=2).unsqueeze(1).to_broadcast([P, n, 2, 2]),
+                op=MULT,
+            )
+            if shared(b):
+                copy_words(dst, bank, 1, 2)
 
         def quantize_qr(b):
             g = live.pop(("gqr", b))
             codes = work.tile([P, 2 * BLOCK], U32, name="cqr", tag="cqr", bufs=3, align_bytes=64)
             scales = work.tile([P, 2 * BLOCK], U8, name="sqr", tag="sqr", bufs=3, align_bytes=64)
-            nc.vector.quantize_mx(out=codes[:].bitcast(FP8X4), scales=scales[:], in_=g[:])
+            nc.vector.quantize_mx(out=codes[:].bitcast(FP8X4), scales=scales[:], in_=g[:].rearrange("p s c -> p (s c)"))
             live["cqr", b] = (codes, scales)
 
         def quantize_z(b):
@@ -191,6 +217,15 @@ def tile_treehopnode_pa_t_kernel(tc, q, rep_bytes, rep_scale, Wq, Wk, Wv, W1, b1
                 for t in range(PACK):
                     mx(bank[:, t, :], key, t, codes, scales, base + unit * UNIT, UNIT)
                 live[key, b, unit] = bank[:].rearrange("p t n -> p n t")
+
+        def project_q(b):
+            project(b, "q")
+
+        def project_k(b):
+            project(b, "k")
+
+        def project_v(b):
+            project(b, "v")
 
         def copy_q(b):
             for unit in range(2):
@@ -221,9 +256,6 @@ def tile_treehopnode_pa_t_kernel(tc, q, rep_bytes, rep_scale, Wq, Wk, Wv, W1, b1
                 nc.vector.tensor_tensor(out=dst, in0=live.pop(("v", b, unit)), in1=t[:, unit, :, :], op=MULT)
             live["gz", b] = z
 
-        def straight(b):
-            return b == BLOCKS - 1
-
         def layer(b):
             codes, scales = live.pop(("cz", b))
             bank = psum.tile([P, 2, BLOCK], F32, name="bank_o", tag="o")
@@ -243,11 +275,12 @@ def tile_treehopnode_pa_t_kernel(tc, q, rep_bytes, rep_scale, Wq, Wk, Wv, W1, b1
             live["o", b] = bank
 
         def add_bias(b):
-            bank = live.pop(("o", b))
+            if not straight(b):
+                return
             t = work.tile([P, 2, M], F32, name="pre", tag="pre", align_bytes=64)
             nc.vector.tensor_tensor(
                 out=t[:].rearrange("p i (m c) -> p i m c", c=2),
-                in0=bank[:].rearrange("p i (c m) -> p i m c", c=2),
+                in0=live.pop(("o", b))[:].rearrange("p i (c m) -> p i m c", c=2),
                 in1=bias_bc[:].rearrange("p i (m c) -> p i m c", c=2),
                 op=mybir.AluOpType.add,
             )
@@ -258,22 +291,24 @@ def tile_treehopnode_pa_t_kernel(tc, q, rep_bytes, rep_scale, Wq, Wk, Wv, W1, b1
             dst = out[first:first + rows * P, :, :].rearrange("(p i) o m -> p i (o m)", p=P)
             nc.sync.dma_start(out=dst[:, i:i + 2, :], in_=t[:])
 
-        def relu_straight(b):
-            t = work.tile([P, 2, M], F32, name="res", tag="res", bufs=3, align_bytes=64)
-            nc.scalar.activation(
-                t[:].rearrange("p i m -> p (i m)"),
-                live.pop(("pre", b))[:].rearrange("p i m -> p (i m)"),
-                ACT.Relu)
-            send(b, t)
-
         def relu(b):
-            bank = live.pop(("o", b))
-            t = work.tile([P, 2, BLOCK], F32, name="act", tag="act", align_bytes=64)
-            for c in range(2):
-                nc.scalar.activation(t[:, c, :], bank[:, c, :], ACT.Relu, bias=bias[:, c:c + 1])
-            live["act", b] = t
+            if straight(b):
+                t = work.tile([P, 2, M], F32, name="res", tag="res", bufs=3, align_bytes=64)
+                nc.scalar.activation(
+                    t[:].rearrange("p i m -> p (i m)"),
+                    live.pop(("pre", b))[:].rearrange("p i m -> p (i m)"),
+                    ACT.Relu)
+                send(b, t)
+            else:
+                bank = live.pop(("o", b))
+                t = work.tile([P, 2, BLOCK], F32, name="act", tag="act", align_bytes=64)
+                for c in range(2):
+                    nc.scalar.activation(t[:, c, :], bank[:, c, :], ACT.Relu, bias=bias[:, c:c + 1])
+                live["act", b] = t
 
         def turn_back(b):
+            if straight(b):
+                return
             t = live.pop(("act", b))
             bank = psum.tile([P, 2, 2, P], F32, name="bank_b", tag="back")
             for i in range(2):
@@ -282,6 +317,8 @@ def tile_treehopnode_pa_t_kernel(tc, q, rep_bytes, rep_scale, Wq, Wk, Wv, W1, b1
             live["back", b] = bank
 
         def store(b):
+            if straight(b):
+                return
             bank = live.pop(("back", b))
             t = work.tile([P, 2, M], F32, name="res", tag="res", bufs=3, align_bytes=64)
             nc.scalar.copy(
@@ -290,62 +327,66 @@ def tile_treehopnode_pa_t_kernel(tc, q, rep_bytes, rep_scale, Wq, Wk, Wv, W1, b1
             )
             send(b, t)
 
-        def on(b):
-            return 0 <= b < BLOCKS
+        done = set()
 
-        for s in range(-4, BLOCKS + 4):
-            if s == -4:
-                weight_group("q", nc.scalar.copy)
-            if on(s):
-                times_k(s)
-            if on(s + 1):
-                project(s + 1, "q")
-            if on(s + 2):
-                collect(s + 2, "q")
-                collect(s + 2, "r")
-            if on(s - 1):
-                times_v(s - 1)
-            if on(s - 2) and straight(s - 2):
-                add_bias(s - 2)
-            if on(s + 3):
-                turn_rep(s + 3)
-            if on(s):
-                gate(s)
-            if on(s + 1):
-                project(s + 1, "k")
-            if on(s + 2):
-                quantize_qr(s + 2)
-            if on(s + 1):
-                copy_q(s + 1)
-            if on(s + 3):
-                turn_q(s + 3)
-            if on(s - 3) and not straight(s - 3):
-                turn_back(s - 3)
-            if on(s):
-                project(s, "v")
-            if on(s - 1):
-                quantize_z(s - 1)
-            if on(s + 4):
-                widen(s + 4)
-            if s == -4:
-                weight_group("k", nc.vector.tensor_copy)
-            if s == -3:
-                weight_quantize("q")
-            if s == -2:
-                weight_quantize("k")
-                weight_group("v", nc.scalar.copy)
-            if s == -1:
-                weight_quantize("v")
+        def do(stage, b):
+            if 0 <= b < BLOCKS and (stage, b) not in done:
+                done.add((stage, b))
+                stage(b)
+
+        spread_scale()
+        do(turn_q, 0)
+        do(collect_q, 0)
+        do(widen, 0)
+        do(turn_rep, 0)
+        weight_group("q", nc.scalar.copy, 0, 2)
+        weight_group("q", nc.vector.tensor_copy, 2, 4)
+        do(turn_q, 1)
+        do(scale_rep, 0)
+        do(collect_q, 1)
+        weight_group("k", nc.scalar.copy)
+        weight_quantize("q")
+        do(widen, 1)
+        do(widen, 2)
+        do(quantize_qr, 0)
+        do(turn_rep, 1)
+        do(project_q, 0)
+        weight_group("v", nc.scalar.copy, 0, 2)
+        weight_group("v", nc.vector.tensor_copy, 2, 4)
+        do(scale_rep, 1)
+        weight_quantize("k")
+        do(turn_rep, 2)
+        do(copy_q, 0)
+        weight_group("1", nc.scalar.copy, 0, 2)
+        do(quantize_qr, 1)
+        do(turn_q, 2)
+        do(project_k, 0)
+        weight_quantize("v")
+        do(widen, 3)
+        STEP = (
+            (scale_rep, 2),
+            (times_k, 0),
+            (collect_q, 2),
+            (times_v, -1),
+            (turn_rep, 3),
+            (project_q, 1),
+            (quantize_qr, 2),
+            (gate, 0),
+            (turn_back, -3),
+            (add_bias, -2),
+            (turn_q, 3),
+            (copy_q, 1),
+            (project_k, 1),
+            (quantize_z, -1),
+            (relu, -2),
+            (store, -3),
+            (project_v, 0),
+            (widen, 4),
+            (layer, -1),
+        )
+        for s in range(BLOCKS + 4):
+            for stage, offset in STEP:
+                do(stage, s + offset)
             if s == 0:
-                weight_group("1", nc.vector.tensor_copy)
                 weight_quantize("1")
                 spread_bias()
-            if on(s - 2):
-                if straight(s - 2):
-                    relu_straight(s - 2)
-                else:
-                    relu(s - 2)
-            if on(s - 1):
-                layer(s - 1)
-            if on(s - 3) and not straight(s - 3):
-                store(s - 3)

from contextlib import ExitStack

import concourse.mybir as mybir
from concourse.masks import make_identity

N, E, G, M = 4096, 512, 512, 256
FLOPS = 2 * N * E * G * 3 + 2 * N * G * M

F32 = mybir.dt.float32
BF16 = mybir.dt.bfloat16
U32 = mybir.dt.uint32
U8 = mybir.dt.uint8
FP8 = mybir.dt.float8_e4m3fn
FP8X4 = mybir.dt.float8_e4m3fn_x4
ACT = mybir.ActivationFunctionType
MULT = mybir.AluOpType.mult

P = 128
PACK = 4
UNIT = 128
BLOCK = 2 * UNIT
BLOCKS = N // BLOCK
GROUPS = (256, 256, 512, 1024, 1024, 1024)


def tile_treehopnode_pa_t_kernel(tc, q, rep_bytes, rep_scale, Wq, Wk, Wv, W1, b1, out):
    nc = tc.nc
    with ExitStack() as ctx:
        keep = ctx.enter_context(tc.tile_pool(name="keep", bufs=1))
        work = ctx.enter_context(tc.tile_pool(name="work", bufs=2))
        psum = ctx.enter_context(tc.psum_pool(name="psum", bufs=1))

        ident = keep.tile([P, P], F32, name="ident")
        make_identity(nc, ident[:])
        warm = keep.tile([P, 1], F32, name="warm")
        nc.vector.memset(warm[:], 0.0)
        warm_out = keep.tile([P, 1], F32, name="warm_out")

        ctx.enter_context(tc.manual_schedule())
        nc.scalar.activation(warm_out[:], warm[:], ACT.Sigmoid)

        scol = keep.tile([P, PACK], F32, name="scol")
        bias = keep.tile([P, 2], BF16, name="bias")
        q_in, r_in, where = [], [], []
        start = 0
        for g, tokens in enumerate(GROUPS):
            rows = tokens // P
            q_in.append(keep.tile([P, rows * E], BF16, name="q_in%d" % g, align_bytes=64))
            r_in.append(keep.tile([P, rows * E], U8, name="r_in%d" % g, align_bytes=64))
            for i in range(0, rows, 2):
                where.append((g, i, start, rows))
            start += tokens

        def load_rep(g):
            first = sum(GROUPS[:g])
            src = rep_bytes[first:first + GROUPS[g], :].rearrange("(p i) k -> p (i k)", p=P)
            nc.sync.dma_start(out=r_in[g][:], in_=src)

        def load_q(g):
            first = sum(GROUPS[:g])
            src = q[first:first + GROUPS[g], :].rearrange("(p i) k -> p (i k)", p=P)
            nc.sync.dma_start(out=q_in[g][:], in_=src)

        raw, grouped, wc, ws = {}, {}, {}, {}

        def load_w(key, src):
            width = src.shape[1]
            raw[key] = keep.tile([P, PACK, width], BF16, name="raw_" + key, align_bytes=64)
            grouped[key] = keep.tile([P, width * PACK], BF16, name="grouped_" + key, align_bytes=64)
            nc.sync.dma_start(out=raw[key][:], in_=src.rearrange("(p j) c -> p j c", j=PACK))

        nc.sync.dma_start(out=scol[:], in_=rep_scale.rearrange("o (p t) -> p (o t)", t=PACK))
        load_rep(0)
        load_q(0)
        load_w("q", Wq)
        load_rep(1)
        load_q(1)
        load_w("k", Wk)
        load_w("v", Wv)
        nc.sync.dma_start(out=bias[:], in_=b1.rearrange("o (p c) -> p (o c)", c=2))
        load_w("1", W1.rearrange("h k m -> (h k) m"))
        for g in range(2, len(GROUPS)):
            load_rep(g)
            load_q(g)

        def weight_group(key, copy, first=0, last=4):
            parts = raw[key].shape[2] // P
            dst = grouped[key][:].rearrange("p (t m j) -> p t m j", t=parts, j=PACK)
            src = raw[key][:].rearrange("p j (m t) -> p t m j", t=parts)
            copy(out=dst[:, first:last, :, :], in_=src[:, first:last, :, :])

        def weight_quantize(key):
            width = raw[key].shape[2]
            wc[key] = keep.tile([P, width], U32, name="wc_" + key, align_bytes=64)
            ws[key] = keep.tile([P, width], U8, name="ws_" + key, align_bytes=64)
            nc.vector.quantize_mx(out=wc[key][:].bitcast(FP8X4), scales=ws[key][:], in_=grouped[key][:])

        def mx(dst, key, col, codes, scales, tok, n):
            nc.tensor.matmul_mx(
                out=dst,
                lhsT=wc[key][:, col * P:(col + 1) * P].bitcast(FP8X4),
                lhsT_scale=ws[key][:, col * P:(col + 1) * P],
                rhs=codes[:, tok:tok + n].bitcast(FP8X4),
                rhs_scale=scales[:, tok:tok + n],
                start=True,
                stop=True,
            )

        sc_bc = keep.tile([P, E], F32, name="sc_bc", align_bytes=64)
        bias_bc = keep.tile([P, 2, M], F32, name="bias_bc", align_bytes=64)
        bias32 = keep.tile([P, 2], F32, name="bias32")

        def spread_scale():
            bank = psum.tile([P, PACK, P], F32, name="bank_sc", tag="back")
            for t in range(PACK):
                nc.tensor.transpose(bank[:, t, :], scol[:, t:t + 1].to_broadcast([P, P]), ident[:])
            nc.vector.tensor_copy(
                out=sc_bc[:].rearrange("p (n t) -> p n t", t=PACK),
                in_=bank[:].rearrange("p t n -> p n t"),
            )

        def spread_bias():
            nc.scalar.copy(out=bias32[:], in_=bias[:])
            bank = psum.tile([P, 2, P], F32, name="bank_bias", tag="back")
            for c in range(2):
                nc.tensor.transpose(bank[:, c, :], bias32[:, c:c + 1].to_broadcast([P, P]), ident[:])
            for i in range(2):
                nc.scalar.copy(
                    out=bias_bc[:, i, :].rearrange("p (m c) -> p m c", c=2),
                    in_=bank[:].rearrange("p c m -> p m c"),
                )

        live = {}

        def shared(b):
            return b in (4,6,8,10,12,14)

        def straight(b):
            return b in (14,15,)

        def widen(b):
            g, i, first, rows = where[b]
            x = work.tile([P, 2 * E], BF16, name="x", tag="x", bufs=3, align_bytes=64)
            for h in range(2):
                dst = x[:, h * E:(h + 1) * E]
                if h == 1 and shared(b):
                    dst = work.tile([P, E], BF16, name="plain", tag="plain", align_bytes=64)[:]
                nc.gpsimd.tensor_copy(out=dst, in_=r_in[g][:, (i + h) * E:(i + h + 1) * E].bitcast(FP8))
            if shared(b):
                for c in range(2):
                    cols = slice(c * E // 2, (c + 1) * E // 2)
                    nc.gpsimd.tensor_tensor(out=x[:, E + c * E // 2:E + (c + 1) * E // 2], in0=dst[:, cols], in1=sc_bc[:, cols], op=MULT)
            live["x", b] = x[:].bitcast(F32)

        def turn(words, tag):
            bank = psum.tile([P, 2, 2, P], F32, name="bank_" + tag, tag=tag)
            half = E // 2
            for i in range(2):
                for u in range(2):
                    nc.tensor.transpose(bank[:, u, i, :], words[:, i * half + u:(i + 1) * half:2], ident[:])
            return bank

        def turn_rep(b):
            live["tr", b] = turn(live.pop(("x", b)), "tr")

        def turn_q(b):
            g, i, first, rows = where[b]
            live["tq", b] = turn(q_in[g][:, i * E:(i + 2) * E].bitcast(F32), "tq")

        def grouped_tile(b):
            if ("gqr", b) not in live:
                live["gqr", b] = work.tile([P, 2, BLOCK * PACK], BF16, name="gqr", tag="gqr", align_bytes=64)
            return live["gqr", b]

        def copy_words(dst, bank, first, last):
            nc.scalar.copy(
                out=dst[:, first * P * PACK:last * P * PACK].bitcast(F32).rearrange("p (i r u) -> p i r u", r=P, u=2),
                in_=bank[:, :, first:last, :].rearrange("p u i r -> p i r u"),
            )

        def collect_q(b):
            copy_words(grouped_tile(b)[:, 0, :], live.pop(("tq", b)), 0, 2)

        def scale_rep(b):
            bank = live.pop(("tr", b))
            dst = grouped_tile(b)[:, 1, :]
            n = P if shared(b) else 2 * P
            words = bank[:].rearrange("p u i r -> p u (i r)")[:, :, 0:n]
            nc.vector.tensor_tensor(
                out=dst[:, 0:n * PACK].rearrange("p (n u e) -> p n u e", u=2, e=2),
                in0=words.bitcast(BF16).rearrange("p u (n e) -> p n u e", e=2),
                in1=scol[:].rearrange("p (u e) -> p u e", e=2).unsqueeze(1).to_broadcast([P, n, 2, 2]),
                op=MULT,
            )
            if shared(b):
                copy_words(dst, bank, 1, 2)

        def quantize_qr(b):
            g = live.pop(("gqr", b))
            codes = work.tile([P, 2 * BLOCK], U32, name="cqr", tag="cqr", bufs=3, align_bytes=64)
            scales = work.tile([P, 2 * BLOCK], U8, name="sqr", tag="sqr", bufs=3, align_bytes=64)
            nc.vector.quantize_mx(out=codes[:].bitcast(FP8X4), scales=scales[:], in_=g[:].rearrange("p s c -> p (s c)"))
            live["cqr", b] = (codes, scales)

        def quantize_z(b):
            g = live.pop(("gz", b))
            codes = work.tile([P, BLOCK], U32, name="cz", tag="cz", align_bytes=64)
            scales = work.tile([P, BLOCK], U8, name="sz", tag="sz", align_bytes=64)
            nc.vector.quantize_mx(out=codes[:].bitcast(FP8X4), scales=scales[:], in_=g[:])
            live["cz", b] = (codes, scales)

        def project(b, key):
            codes, scales = live["cqr", b]
            base = 0 if key == "q" else BLOCK
            for unit in range(2):
                bank = psum.tile([P, PACK, UNIT], F32, name="bank_qkv", tag="qkv", bufs=4)
                for t in range(PACK):
                    mx(bank[:, t, :], key, t, codes, scales, base + unit * UNIT, UNIT)
                live[key, b, unit] = bank[:].rearrange("p t n -> p n t")

        def project_q(b):
            project(b, "q")

        def project_k(b):
            project(b, "k")

        def project_v(b):
            project(b, "v")

        def copy_q(b):
            for unit in range(2):
                t = work.tile([P, UNIT, PACK], F32, name="q_sb", tag="q_sb", bufs=4, align_bytes=64)
                nc.scalar.copy(out=t[:], in_=live.pop(("q", b, unit)))
                live["qs", b, unit] = t

        def times_k(b):
            t = work.tile([P, 2, UNIT, PACK], F32, name="qk", tag="qk", align_bytes=64)
            for unit in range(2):
                nc.vector.tensor_tensor(out=t[:, unit, :, :], in0=live.pop(("k", b, unit)), in1=live.pop(("qs", b, unit))[:], op=MULT)
            live["qk", b] = t

        def gate(b):
            t = work.tile([P, 2, UNIT, PACK], F32, name="gate", tag="gate", align_bytes=64)
            nc.scalar.activation(
                t[:].rearrange("p i n t -> p (i n t)"),
                live.pop(("qk", b))[:].rearrange("p i n t -> p (i n t)"),
                ACT.Sigmoid, scale=G ** -0.5)
            live["gate", b] = t

        def times_v(b):
            z = work.tile([P, BLOCK * PACK], BF16, name="gz", tag="gz", align_bytes=64)
            t = live.pop(("gate", b))
            half = UNIT * PACK
            for unit in range(2):
                dst = z[:, unit * half:(unit + 1) * half].rearrange("p (n t) -> p n t", t=PACK)
                nc.vector.tensor_tensor(out=dst, in0=live.pop(("v", b, unit)), in1=t[:, unit, :, :], op=MULT)
            live["gz", b] = z

        def layer(b):
            codes, scales = live.pop(("cz", b))
            bank = psum.tile([P, 2, BLOCK], F32, name="bank_o", tag="o")
            for c in range(2):
                if straight(b):
                    nc.tensor.matmul_mx(
                        out=bank[:, c, :],
                        lhsT=codes[:, c * UNIT:(c + 1) * UNIT].bitcast(FP8X4),
                        lhsT_scale=scales[:, c * UNIT:(c + 1) * UNIT],
                        rhs=wc["1"][:].bitcast(FP8X4),
                        rhs_scale=ws["1"][:],
                        start=True,
                        stop=True,
                    )
                else:
                    mx(bank[:, c, :], "1", c, codes, scales, 0, BLOCK)
            live["o", b] = bank

        def add_bias(b):
            if not straight(b):
                return
            t = work.tile([P, 2, M], F32, name="pre", tag="pre", align_bytes=64)
            nc.vector.tensor_tensor(
                out=t[:].rearrange("p i (m c) -> p i m c", c=2),
                in0=live.pop(("o", b))[:].rearrange("p i (c m) -> p i m c", c=2),
                in1=bias_bc[:].rearrange("p i (m c) -> p i m c", c=2),
                op=mybir.AluOpType.add,
            )
            live["pre", b] = t

        def send(b, t):
            g, i, first, rows = where[b]
            dst = out[first:first + rows * P, :, :].rearrange("(p i) o m -> p i (o m)", p=P)
            nc.sync.dma_start(out=dst[:, i:i + 2, :], in_=t[:])

        def relu(b):
            if straight(b):
                t = work.tile([P, 2, M], F32, name="res", tag="res", bufs=3, align_bytes=64)
                nc.scalar.activation(
                    t[:].rearrange("p i m -> p (i m)"),
                    live.pop(("pre", b))[:].rearrange("p i m -> p (i m)"),
                    ACT.Relu)
                send(b, t)
            else:
                bank = live.pop(("o", b))
                t = work.tile([P, 2, BLOCK], F32, name="act", tag="act", align_bytes=64)
                for c in range(2):
                    nc.scalar.activation(t[:, c, :], bank[:, c, :], ACT.Relu, bias=bias[:, c:c + 1])
                live["act", b] = t

        def turn_back(b):
            if straight(b):
                return
            t = live.pop(("act", b))
            bank = psum.tile([P, 2, 2, P], F32, name="bank_b", tag="back")
            for i in range(2):
                for c in range(2):
                    nc.tensor.transpose(bank[:, i, c, :], t[:, c, i * UNIT:(i + 1) * UNIT], ident[:])
            live["back", b] = bank

        def store(b):
            if straight(b):
                return
            bank = live.pop(("back", b))
            t = work.tile([P, 2, M], F32, name="res", tag="res", bufs=3, align_bytes=64)
            nc.scalar.copy(
                out=t[:].rearrange("p i (m c) -> p i m c", c=2),
                in_=bank[:].rearrange("p i c m -> p i m c"),
            )
            send(b, t)

        done = set()

        def do(stage, b):
            if 0 <= b < BLOCKS and (stage, b) not in done:
                done.add((stage, b))
                stage(b)

        spread_scale()
        do(turn_q, 0)
        do(collect_q, 0)
        do(widen, 0)
        do(turn_rep, 0)
        weight_group("q", nc.scalar.copy, 0, 2)
        weight_group("q", nc.vector.tensor_copy, 2, 4)
        do(turn_q, 1)
        do(scale_rep, 0)
        do(collect_q, 1)
        weight_group("k", nc.scalar.copy)
        weight_quantize("q")
        do(widen, 1)
        do(widen, 2)
        do(quantize_qr, 0)
        do(turn_rep, 1)
        do(project_q, 0)
        weight_group("v", nc.scalar.copy, 0, 2)
        weight_group("v", nc.vector.tensor_copy, 2, 4)
        do(scale_rep, 1)
        weight_quantize("k")
        do(turn_rep, 2)
        do(copy_q, 0)
        weight_group("1", nc.scalar.copy, 0, 2)
        do(quantize_qr, 1)
        do(turn_q, 2)
        do(project_k, 0)
        weight_quantize("v")
        do(widen, 3)
        STEP = (
            (scale_rep, 2),
            (times_k, 0),
            (collect_q, 2),
            (times_v, -1),
            (turn_rep, 3),
            (project_q, 1),
            (quantize_qr, 2),
            (gate, 0),
            (turn_back, -3),
            (add_bias, -2),
            (turn_q, 3),
            (copy_q, 1),
            (project_k, 1),
            (quantize_z, -1),
            (relu, -2),
            (store, -3),
            (project_v, 0),
            (widen, 4),
            (layer, -1),
        )
        for s in range(BLOCKS + 4):
            for stage, offset in STEP:
                do(stage, s + offset)
            if s == 0:
                weight_quantize("1")
                spread_bias()
